import numpy as np
import ml_dtypes


def mxq(x, axis, fmt="e4m3"):
    dtype, down = {"e4m3": (ml_dtypes.float8_e4m3fn, 7), "e5m2": (ml_dtypes.float8_e5m2, 14)}[fmt]
    v = np.moveaxis(np.asarray(x, np.float32).astype(ml_dtypes.bfloat16).astype(np.float64), axis, -1)
    blocks = v.reshape(v.shape[:-1] + (-1, 32))
    amax = np.abs(blocks).max(-1, keepdims=True)
    byte = np.maximum(np.where(amax > 0, np.frexp(amax)[1] - 1 + 127, 0) - down, 1)
    scale = np.exp2(byte - 127.0)
    codes = (blocks / scale).astype(np.float32).astype(dtype).astype(np.float64)
    return np.moveaxis((codes * scale).reshape(v.shape), -1, axis)


WIDE = False


def mx_kscale(k):
    if not WIDE:
        return np.ones(k)
    levels = np.array([18, -18])
    if k % 512:
        return np.exp2(np.random.permutation(np.resize(levels, k // 32))).repeat(32)
    a = np.empty((k // 512, 16))
    for p in range(k // 512):
        a[p, :8] = np.random.permutation(np.resize(levels, 8))
        for g in range(8):
            far = levels[np.abs(levels - a[p, g]) >= 10]
            a[p, g + 8] = far[np.random.randint(len(far))]
    return np.exp2(a.ravel()).repeat(32)


BF16 = ml_dtypes.bfloat16


def bf(x):
    return np.asarray(x, np.float32).astype(BF16)


def f64(x):
    return np.asarray(x).astype(np.float64)


L, N, E, H, C, LW, RW = 2048, 1, 512, 1, 512, 1, 1
DH = E // H
W = L // C


def seen(w):
    return max(w - LW, 0) * C, min(w + RW + 1, W) * C


def setup_inputs():
    u = mx_kscale(DH)
    t = mx_kscale(L)[:, None]
    s = mx_kscale(L)[:, None]
    q0 = bf(np.random.standard_normal((N * H, L, DH)) / np.sqrt(DH))
    k0 = bf(np.random.standard_normal((N * H, L, DH)) * 0.5)
    v0 = bf(np.random.standard_normal((N * H, L, DH)) * 0.125)
    g = bf(np.random.standard_normal((N * H, L, DH)) * np.exp2(np.random.randint(-6, 1, (N * H, L, 1))) / s * u)
    dots = []
    for w in range(W):
        lo, hi = seen(w)
        z = f64(q0)[:, w * C:(w + 1) * C] @ f64(k0)[:, lo:hi].transpose(0, 2, 1)
        dots.append(np.asarray(z, np.float32))
    return {"q_scaled": bf(f64(q0) * s), "k_heads": bf(f64(k0) / t), "v_heads": bf(f64(v0) * t / u),
            "dots_0": dots[0], "dots_1": dots[1], "dots_2": dots[2], "dots_3": dots[3], "grad_out": g}


def reference(q_scaled, k_heads, v_heads, dots_0, dots_1, dots_2, dots_3, grad_out):
    dots = [f64(dots_0), f64(dots_1), f64(dots_2), f64(dots_3)]
    gq = mxq(f64(grad_out), 2, "e5m2")
    vq = mxq(f64(v_heads), 2, "e4m3")
    kq = mxq(f64(k_heads), 1, "e4m3")
    qq = mxq(f64(q_scaled), 1, "e4m3")
    dz1, dq, dk = [], [], []
    for w in range(W):
        lo, hi = seen(w)
        dh = gq[:, w * C:(w + 1) * C] @ vq[:, lo:hi].transpose(0, 2, 1)
        d = dh * (dots[w] > 0.0)
        dz1.append(d)
        dq.append(mxq(d, 2, "e5m2") @ kq[:, lo:hi])
    for j in range(W):
        a, b = max(j - RW, 0), min(j + LW + 1, W)
        d = np.concatenate([dz1[w][:, :, j * C - seen(w)[0]:(j + 1) * C - seen(w)[0]] for w in range(a, b)], axis=1)
        dk.append(mxq(d, 1, "e5m2").transpose(0, 2, 1) @ qq[:, a * C:b * C])
    return np.concatenate(dq, axis=1), np.concatenate(dk, axis=1)

from contextlib import ExitStack
import concourse.mybir as mybir
from concourse.masks import make_identity

FLOPS = 120 * 2 * 512 * 128 * 512

F32 = mybir.dt.float32
BF16 = mybir.dt.bfloat16
U32 = mybir.dt.uint32
U8 = mybir.dt.uint8
E4 = mybir.dt.float8_e4m3fn_x4
E5 = mybir.dt.float8_e5m2_x4
ALU = mybir.AluOpType

P = 128
C = 512
W = 4
D = 512
PAIRS = [(w, j) for w in range(W) for j in range(max(w - 1, 0), min(w + 2, W))]
N = len(PAIRS)
DOTS_BUFS=5; TR_BUFS=2; DH_BUFS=4; O_BUFS=2
LO=[('v',0,2),('g',0,2),('d',0,4),('v',1,1),('d',1,2),('g',1,1),('k',0,1),('d',2,1),('k',1,1),('d',3,1),('q',0,1),('q',1,1),('v',2,1),('g',2,1),('d',4,1),('d',5,1),('k',2,1),('d',6,1),('q',2,1),('v',3,1),('g',3,1),('d',7,1),('d',8,1),('k',3,1),('d',9,1),('q',3,1)]
UPTO={-1:11,0:13,1:15,2:17,3:19,4:22,5:24,6:26}
TRP={0:[('g',1)],1:[('v',2)],2:[('g',2)],4:[('v',3)],5:[('g',3)]}
QP={0:[('g',1)],2:[('v',2)],3:[('g',2)],5:[('v',3)],6:[('g',3)]}
IL={-1:[('k',0),('k',1)],1:[('q',0),('q',1)],4:[('k',2)],5:[('q',2)],6:[('k',3)],7:[('q',3)]}
QK={2:[('k',0),('k',1)],3:[('q',0),('q',1)],5:[('k',2)],6:[('q',2)],7:[('k',3)],8:[('q',3)]}
OG={3:(0,0),5:(1,0),6:(0,1),7:(1,1),9:(0,2)}
ILV="SVSVSVSVV"
KQE = "GGGGGGGGGGGGGGGG"
KP = 2


def tile_normlocalattention_pa_v_kernel(tc, q_scaled, k_heads, v_heads, dots_0, dots_1, dots_2, dots_3, grad_out, out_0, out_1):
    nc = tc.nc
    dots = [dots_0, dots_1, dots_2, dots_3]
    src = {"q": q_scaled, "k": k_heads, "v": v_heads, "g": grad_out}
    with ExitStack() as ctx:
        const = ctx.enter_context(tc.tile_pool(name="const", bufs=1))
        rawp = ctx.enter_context(tc.tile_pool(name="raw", bufs=2))
        work = ctx.enter_context(tc.tile_pool(name="work", bufs=3))
        keep = ctx.enter_context(tc.tile_pool(name="keep", bufs=1))
        outp = ctx.enter_context(tc.tile_pool(name="outp", bufs=6))
        psum = ctx.enter_context(tc.psum_pool(name="psum", bufs=2))

        ident = const.tile([P, P], F32, name="ident")
        make_identity(nc, ident[:])

        raw, grp, codes, scales, dts, dhp, trp, dz, zT, zI = {}, {}, {}, {}, {}, {}, {}, {}, {}, {}
        zTq, zTs, zIq, zIs, ob, ot = {}, {}, {}, {}, {}, {}

        def copy(eng, out, in_):
            if eng == "G":
                nc.gpsimd.tensor_scalar(out=out, in0=in_, scalar1=1.0, scalar2=0.0, op0=ALU.mult, op1=ALU.add)
            elif eng == "V":
                nc.vector.tensor_copy(out=out, in_=in_)
            else:
                nc.scalar.copy(out=out, in_=in_)

        def load_raw(a, c, parts=1):
            t = rawp.tile([P, 4, D], BF16, name="raw_" + a, bufs=2)
            raw[a, c] = t
            v = src[a][0, C * c : C * (c + 1), :].rearrange("(p t) d -> p t d", t=4)
            for i in range(parts):
                s = slice(4 * i // parts, 4 * (i + 1) // parts)
                nc.sync.dma_start(out=t[:, s, :], in_=v[:, s, :])

        def load_dots(n, parts=1):
            w, j = PAIRS[n]
            t = rawp.tile([P, 4, C], F32, name="dots", bufs=DOTS_BUFS)
            dts[n] = t
            k0 = C * (j - max(w - 1, 0))
            v = dots[w][0, :, k0 : k0 + C].rearrange("(p t) k -> p t k", t=4)
            for i in range(parts):
                s = slice(4 * i // parts, 4 * (i + 1) // parts)
                nc.sync.dma_start(out=t[:, s, :], in_=v[:, s, :])

        def tr_raw(a, c, half):
            b = psum.tile([P, 2, 2, P], F32, name="tr", bufs=TR_BUFS)
            trp[a, c, half] = b
            words = raw[a, c][:].rearrange("p t d -> p (t d)").bitcast(F32).rearrange("p (t w) -> p t w", t=4)
            for i in range(2):
                for u in range(2):
                    nc.tensor.transpose(b[:, i, u, :], words[:, (half + 2 * i) if a == "v" else (2 * half + i), u :: 2], ident[:])

        def cp_raw(a, c, half, eng):
            if (a, c) not in grp:
                grp[a, c] = work.tile([P, C * 4], BF16, name="grp_" + a, bufs=2, align_bytes=64)
            g = grp[a, c][:].bitcast(F32)
            b = trp[a, c, half]
            if a == "v":
                dst = g.rearrange("p (k r t u) -> p k r t u", k=2, t=2, u=2)[:, half, :, :, :]
                copy(eng, dst, b[:].rearrange("p t u r -> p r t u"))
            else:
                dst = g.rearrange("p (t r u) -> p t r u", t=4, u=2)[:, 2 * half : 2 * half + 2, :, :]
                copy(eng, dst, b[:].rearrange("p t u r -> p t r u"))

        def il_raw(a, c, part, eng, parts=2):
            if (a, c) not in grp:
                grp[a, c] = work.tile([P, C * 4], BF16, name="grp_kq", bufs=3, align_bytes=64)
            w = D // parts
            s = slice(w * part, w * part + w)
            d = grp[a, c][:, 4 * w * part : 4 * w * (part + 1)]
            if a == "k":
                copy(eng, d.rearrange("p (c u e) -> p c u e", u=2, e=2), raw[a, c][:].rearrange("p (e u) d -> p e u d", e=2)[:, :, :, s].rearrange("p e u c -> p c u e"))
            elif eng == "G":
                copy(eng, d.rearrange("p (c t) -> p c t", t=4), raw[a, c][:, :, s].rearrange("p t c -> p c t"))
            else:
                copy(eng, d.rearrange("p (c i t) -> p c t i", i=4, t=4), raw[a, c][:, :, s].rearrange("p t (c i) -> p c t i", i=4))

        def quant(a, c, part=0, parts=1):
            if (a, c) not in codes:
                codes[a, c] = keep.tile([P, D], U32, name="codes_%s%d" % (a, c), align_bytes=64)
                scales[a, c] = keep.tile([P, D], U8, name="scales_%s%d" % (a, c), align_bytes=64)
            w = D // parts
            s = slice(w * part, w * part + w)
            nc.vector.quantize_mx(out=codes[a, c][:, s].bitcast(E5 if a == "g" else E4), scales=scales[a, c][:, s], in_=grp[a, c][:, 4 * w * part : 4 * w * (part + 1)])

        def mm(out, lq, ls, lf, cols, rq, rs, rf, start, stop):
            nc.tensor.matmul_mx(out=out, lhsT=lq[:, cols].bitcast(lf), lhsT_scale=ls[:, cols], rhs=rq[:].bitcast(rf), rhs_scale=rs[:], start=start, stop=stop)

        def dh(n, t):
            w, j = PAIRS[n]
            b = psum.tile([P, C], F32, name="dh", bufs=DH_BUFS)
            dhp[n, t] = b
            mm(b[:], codes["g", w], scales["g", w], E5, slice(P * t, P * t + P), codes["v", j], scales["v", j], E4, True, True)

        def mask(n, t, u=None):
            if n not in dz:
                dz[n] = work.tile([P, 4, C], BF16, name="dz", bufs=3)
            s = slice(0, 2) if u is None else slice(u, u + 1)
            nc.vector.scalar_tensor_tensor(out=dz[n][:, t, :].rearrange("p (u x) -> p u x", u=2)[:, s, :], in0=dts[n][:, t, :].rearrange("p (x u) -> p u x", u=2)[:, s, :], scalar=0.0, in1=dhp[n, t][:].rearrange("p (u x) -> p u x", u=2)[:, s, :], op0=ALU.is_gt, op1=ALU.mult)

        def tr_z(n, half):
            b = psum.tile([P, 2, 2, P], F32, name="tr", bufs=TR_BUFS)
            trp["z", n, half] = b
            words = dz[n][:].rearrange("p t d -> p (t d)").bitcast(F32).rearrange("p (t w) -> p t w", t=4)
            for i in range(2):
                for u in range(2):
                    nc.tensor.transpose(b[:, i, u, :], words[:, 2 * half + i, P * u : P * u + P], ident[:])

        def cp_z(n, half, eng):
            if n not in zT:
                zT[n] = work.tile([P, C * 4], BF16, name="zT", bufs=3, align_bytes=64)
            dst = zT[n][:].bitcast(F32).rearrange("p (t r u) -> p t r u", t=4, u=2)[:, 2 * half : 2 * half + 2, :, :]
            copy(eng, dst, trp["z", n, half][:].rearrange("p t u r -> p t r u"))

        def il_z(n, half, eng):
            if n not in zI:
                zI[n] = work.tile([P, C * 4], BF16, name="zI", bufs=3, align_bytes=64)
            s = slice(256 * half, 256 * half + 256)
            dst = zI[n][:, 4 * 256 * half : 4 * 256 * (half + 1)].rearrange("p (c i t) -> p c t i", i=4, t=4)
            copy(eng, dst, dz[n][:, :, s].rearrange("p t (c i) -> p c t i", i=4))

        def quant_z(n, which, part=0, parts=1):
            z, qd, sd, b = (zT, zTq, zTs, 4) if which == "T" else (zI, zIq, zIs, 7)
            if n not in qd:
                qd[n] = work.tile([P, C], U32, name="z%sq" % which, bufs=b, align_bytes=64)
                sd[n] = work.tile([P, C], U8, name="z%ss" % which, bufs=b, align_bytes=64)
            w = C // parts
            s = slice(w * part, w * part + w)
            nc.vector.quantize_mx(out=qd[n][:, s].bitcast(E5), scales=sd[n][:, s], in_=z[n][:, 4 * w * part : 4 * w * (part + 1)])

        def og(o, c, t, last=None, tag="o"):
            ns = [n for n in range(N) if PAIRS[n][o] == c]
            if last is not True:
                ob[o, c, t] = psum.tile([P, D], F32, name=tag, bufs={"o": O_BUFS, "dh": DH_BUFS, "tr": TR_BUFS}[tag])
            b = ob[o, c, t]
            for n in ns if last is None else (ns[-1:] if last else ns[:-1]):
                other = PAIRS[n][1 - o]
                a = "k" if o == 0 else "q"
                qd, sd = (zTq, zTs) if o == 0 else (zIq, zIs)
                mm(b[:], qd[n], sd[n], E5, slice(P * t, P * t + P), codes[a, other], scales[a, other], E4, n == ns[0], n == ns[-1])

        def ev(o, c, t, eng, grain=2):
            g, i = (t // 2, t % 2) if o == 0 else (t % 2, t // 2)
            if i % grain == 0:
                ot[o, c, g] = outp.tile([P, 2, D], F32, name="ot", bufs=6)
            k = i % grain
            copy(eng, ot[o, c, g][:, k, :], ob[o, c, t][:])
            if k == grain - 1:
                rows = [out_0, out_1][o][0, C * c : C * (c + 1), :]
                if o == 0:
                    dst = rows.rearrange("(p t) d -> p t d", t=4)[:, t + 1 - grain : t + 1, :]
                else:
                    dst = rows[256 * g : 256 * g + 256, :].rearrange("(m u) d -> m u d", u=2)[:, i + 1 - grain : i + 1, :]
                nc.sync.dma_start(out=dst, in_=ot[o, c, g][:, 0:grain, :])

        li=[0]; ki=[0]
        def loads(n):
            while li[0]<UPTO.get(n,0):
                a,c,p=LO[li[0]]; li[0]+=1
                (load_dots(c,p) if a=='d' else load_raw(a,c,p))
        def kq_il(a,c):
            for h in range(KP):
                il_raw(a,c,h,KQE[ki[0]*2//KP],KP); ki[0]+=1
        loads(-1)
        for h in (0,1):
            tr_raw('v',0,h); cp_raw('v',0,h,'SV'[h])
        quant('v',0)
        for h in (0,1):
            tr_raw('g',0,h); cp_raw('g',0,h,'SS'[h]); quant('g',0,h,2)
            for t in (0,1): dh(0,2*h+t)
        for h in (0,1): tr_raw('v',1,h); cp_raw('v',1,h,'S')
        for a,c in IL[-1]: kq_il(a,c)
        for n in range(N):
            loads(n)
            m=n-1
            gs=[OG[n]+(t,) for t in range(4)] if n in OG else []
            def o(k):
                if k<len(gs): og(*gs[k])
            def e(k,eng='S'):
                if k<len(gs): ev(*gs[k],eng)
            if n<9:
                for t in range(4):
                    if n==0 and t==2: quant('v',1)
                    mask(n,t)
            else:
                mask(9,0); mask(9,1); tr_z(9,0); cp_z(9,0,'S'); quant_z(8,'T'); quant_z(9,'T',0,2)
                mask(9,2,0); mask(9,3,0); il_z(9,0,'V'); mask(9,2,1); mask(9,3,1); quant_z(9,'I',0,2); tr_z(9,1); cp_z(9,1,'S'); il_z(9,1,'V')
            if m>=0: il_z(m,1,'S')
            for t in range(4):
                o(t); e(t)
                if n+1<N: dh(n+1,t)
            if m>=0: il_z(m,0,ILV[m])
            if m>=0 and m!=8: quant_z(m,'T')
            if n>0:
                for a,c in QP.get(n,[]): quant(a,c)
            for a,c in QK.get(n,[]): quant(a,c)
            if m>=0: quant_z(m,'I')
            if n<9:
                tr_z(n,0);tr_z(n,1)
                cp_z(n,0,'S');cp_z(n,1,'S')
            for a,c in TRP.get(n,[]):
                for h in (0,1): tr_raw(a,c,h); cp_raw(a,c,h,'S')
            if n==0: quant('g',1)
            for a,c in IL.get(n,[]): kq_il(a,c)
        for t in range(2): og(0,3,t,None,'dh'); ev(0,3,t,'S',1)
        for t in range(4): og(1,2,t); ev(1,2,t,'S')
        for t in range(2): og(1,3,t,None,'dh'); ev(1,3,t,'S',1)
        quant_z(9,'T',1,2); quant_z(9,'I',1,2)
        for t in range(2,4): og(0,3,t,None,'dh'); ev(0,3,t,'VS'[t%2],1)
        for t in range(2,4): og(1,3,t,None,'dh'); ev(1,3,t,'VS'[t%2],1)
